import numpy as np
import ml_dtypes


def mxq(x, axis, fmt="e4m3"):
    dtype, down = {"e4m3": (ml_dtypes.float8_e4m3fn, 7), "e5m2": (ml_dtypes.float8_e5m2, 14)}[fmt]
    v = np.moveaxis(np.asarray(x, np.float32).astype(ml_dtypes.bfloat16).astype(np.float64), axis, -1)
    blocks = v.reshape(v.shape[:-1] + (-1, 32))
    amax = np.abs(blocks).max(-1, keepdims=True)
    byte = np.maximum(np.where(amax > 0, np.frexp(amax)[1] - 1 + 127, 0) - down, 1)
    scale = np.exp2(byte - 127.0)
    codes = (blocks / scale).astype(np.float32).astype(dtype).astype(np.float64)
    return np.moveaxis((codes * scale).reshape(v.shape), -1, axis)


WIDE = False


def mx_kscale(k):
    if not WIDE:
        return np.ones(k)
    levels = np.array([30, -30])
    if k % 512:
        return np.exp2(np.random.permutation(np.resize(levels, k // 32))).repeat(32)
    a = np.empty((k // 512, 16))
    for p in range(k // 512):
        a[p, :8] = np.random.permutation(np.resize(levels, 8))
        for g in range(8):
            far = levels[np.abs(levels - a[p, g]) >= 10]
            a[p, g + 8] = far[np.random.randint(len(far))]
    return np.exp2(a.ravel()).repeat(32)


BF16 = ml_dtypes.bfloat16


def bf(x):
    return np.asarray(x, np.float32).astype(BF16)


def f64(x):
    return np.asarray(x).astype(np.float64)


B, S, H, NH = 4, 256, 1024, 16
DK = H // NH
NORM_EPS = 1e-6


def elu(v):
    return np.where(v > 0.0, v, np.exp(np.minimum(v, 0.0)) - 1.0)


def setup_inputs():
    s = mx_kscale(H)
    w = 1.0 / np.sqrt(H)
    return {"hidden_states": bf(np.random.standard_normal((B, S, H)) * s),
            "Wq": bf(np.random.standard_normal((H, H)) * 1.5 * w / s[:, None]),
            "Wk": bf(np.random.standard_normal((H, H)) * 1.5 * w / s[:, None]),
            "Wv": bf(np.random.standard_normal((H, H)) * 2.0 * w / s[:, None])}


def reference(hidden_states, Wq, Wk, Wv):
    xq = mxq(f64(hidden_states), 2, "e5m2")
    q = (xq @ mxq(f64(Wq), 0, "e4m3")).reshape(B, S, NH, DK)
    k = (xq @ mxq(f64(Wk), 0, "e4m3")).reshape(B, S, NH, DK)
    v = (xq @ mxq(f64(Wv), 0, "e4m3")).reshape(B, S, NH, DK)
    q = elu(q) + 1.0
    k = elu(k) + 1.0
    qk = np.sum(q * k, axis=-1, keepdims=True)
    k_sum = np.sum(k, axis=1, keepdims=True)
    normalizer = np.sum(q * k_sum, axis=-1, keepdims=True)
    z = qk * v / (normalizer + NORM_EPS)
    return z.reshape(B, S, H)

@@ -1,0 +1,365 @@
+from contextlib import ExitStack
+
+import concourse.mybir as mybir
+from concourse.masks import make_identity
+
+B, S, H, NH = 4, 256, 1024, 16
+DK = H // NH
+NORM_EPS = 1e-6
+TOKENS = B * S
+FLOPS = 3 * 2 * TOKENS * H * H
+
+F32 = mybir.dt.float32
+BF16 = mybir.dt.bfloat16
+U32 = mybir.dt.uint32
+U8 = mybir.dt.uint8
+E4M3 = mybir.dt.float8_e4m3fn_x4
+E5M2 = mybir.dt.float8_e5m2_x4
+ACT = mybir.ActivationFunctionType
+ALU = mybir.AluOpType
+
+P = 128
+PACK = 4
+K_PASS = P * PACK
+PASSES = H // K_PASS
+GROUP = 256
+GROUPS = H // GROUP
+HALF = 512
+SUM_LAG = 3
+VALUE_LAG = 7
+PREP_RATE = 5
+PREP_HEAD = 2
+FIRST_VECTOR_BANK = 8
+VMOD = 1
+G_FROM = 0
+G_TO = 0
+PROJ_BANKS = 4
+WEAVE = True
+SCALAR_PIECES = 4
+SCALAR_FROM = 3
+
+
+def tile_gatedlinearattention_pa_kernel(tc, hidden_states, Wq, Wk, Wv, out):
+    nc = tc.nc
+    x = hidden_states.rearrange("b s h -> (b s) h")
+    z_out = out.rearrange("b s h -> (b s) h")
+    weights = {"q": Wq, "k": Wk, "v": Wv}
+
+    with ExitStack() as ctx:
+        keep = ctx.enter_context(tc.tile_pool(name="keep", bufs=1))
+        stage = ctx.enter_context(tc.tile_pool(name="stage", bufs=4))
+        work = ctx.enter_context(tc.tile_pool(name="work", bufs=6))
+        proj_psum = ctx.enter_context(tc.psum_pool(name="proj", bufs=PROJ_BANKS))
+        value_psum = ctx.enter_context(tc.psum_pool(name="value", bufs=2))
+        sum_psum = ctx.enter_context(tc.psum_pool(name="sums", bufs=6 - PROJ_BANKS))
+        ctx.enter_context(tc.manual_schedule())
+
+        identity = keep.tile([P, P], F32, name="identity")
+        make_identity(nc, identity[:])
+        head_mask = keep.tile([P, 2], F32, name="head_mask")
+        nc.gpsimd.memset(head_mask[:], 0.0)
+        nc.gpsimd.memset(head_mask[0:DK, 0:1], 1.0)
+        nc.gpsimd.memset(head_mask[DK:P, 1:2], 1.0)
+
+        x_codes = keep.tile([P, PASSES, TOKENS], U32, name="x_codes", align_bytes=64)
+        x_scales = keep.tile([P, PASSES, TOKENS], U8, name="x_scales", align_bytes=64)
+        w_codes, w_scales = {}, {}
+        for w in "kqv":
+            w_codes[w] = keep.tile([P, PASSES, H], U32, name="codes_" + w, align_bytes=64)
+            w_scales[w] = keep.tile([P, PASSES, H], U8, name="scales_" + w, align_bytes=64)
+
+        x_raw, w_raw, w_grouped, x_grouped = {}, {}, {}, {}
+
+        def load_x(t):
+            x_raw[t] = keep.tile([P, H], BF16, name="x_raw_%d" % t, align_bytes=64)
+            nc.sync.dma_start(out=x_raw[t][:], in_=x[t * P:(t + 1) * P, :])
+
+        def load_w(piece):
+            w, g, c = piece
+            w_raw[piece] = keep.tile([P, PACK, GROUP], BF16, name="raw_%s_%d_%d" % piece, align_bytes=64)
+            rows = weights[w][c * K_PASS:(c + 1) * K_PASS, g * GROUP:(g + 1) * GROUP]
+            nc.sync.dma_start(out=w_raw[piece][:], in_=rows.rearrange("(p j) n -> p j n", j=PACK))
+
+        def interleave_w(piece, on_scalar_engine=False):
+            w_grouped[piece] = stage.tile([P, GROUP, PACK], BF16, name="w_grouped", align_bytes=64)
+            copy = nc.scalar.copy if on_scalar_engine else nc.vector.tensor_copy
+            copy(out=w_grouped[piece][:], in_=w_raw[piece][:].rearrange("p j n -> p n j"))
+
+        def quantize_w(piece):
+            w, g, c = piece
+            cols = slice(g * GROUP, (g + 1) * GROUP)
+            nc.vector.quantize_mx(
+                out=w_codes[w][:, c, cols].bitcast(E4M3),
+                scales=w_scales[w][:, c, cols],
+                in_=w_grouped[piece][:].rearrange("p n j -> p (n j)"),
+            )
+
+        def turn_x(t):
+            bank = value_psum.tile([P, PASSES, 2, P], F32, name="value_bank")
+            words = x_raw[t][:].bitcast(F32)
+            for c in range(PASSES):
+                for u in range(2):
+                    nc.tensor.transpose(bank[:, c, u, :], words[:, 256 * c + u:256 * (c + 1):2], identity[:])
+            return bank
+
+        def copy_x(t, bank):
+            pair = t // 2
+            if t % 2 == 0:
+                x_grouped[pair] = stage.tile([P, PASSES, 2, P, 2], F32, name="x_grouped", align_bytes=64)
+            nc.scalar.copy(out=x_grouped[pair][:, :, t % 2, :, :], in_=bank[:].rearrange("p c u r -> p c r u"))
+
+        def quantize_x(pair, c):
+            cols = slice(pair * 2 * P, (pair + 1) * 2 * P)
+            nc.vector.quantize_mx(
+                out=x_codes[:, c, cols].bitcast(E5M2),
+                scales=x_scales[:, c, cols],
+                in_=x_grouped[pair][:, c, :, :, :].rearrange("p t r u -> p (t r u)").bitcast(BF16),
+            )
+
+        units = []
+        for g in range(GROUPS):
+            for half in range(TOKENS // HALF):
+                if (g, half) in ((0, 0), (GROUPS - 1, 1)):
+                    units += [(g, half * HALF, S), (g, half * HALF + S, S)]
+                else:
+                    units.append((g, half * HALF, HALF))
+        steps = 2 * len(units)
+        banks = [(u, b) for u in range(len(units)) for b in range(units[u][2] // S)]
+
+        def step_place(s):
+            g, tok, width = units[s // 2]
+            return g * GROUP + (s % 2) * P, tok, width
+
+        proj, exp_part, feature, k_sum, k_sum_heads, product = {}, {}, {}, {}, {}, {}
+        sums, ratio, value = {}, {}, {}
+
+        def project_pass(w, s, c):
+            col, tok, width = step_place(s)
+            if c == 0:
+                proj[w, s] = proj_psum.tile([P, width], F32, name="proj_bank")
+            nc.tensor.matmul_mx(
+                out=proj[w, s][:],
+                lhsT=w_codes[w][:, c, col:col + P].bitcast(E4M3),
+                lhsT_scale=w_scales[w][:, c, col:col + P],
+                rhs=x_codes[:, c, tok:tok + width].bitcast(E5M2),
+                rhs_scale=x_scales[:, c, tok:tok + width],
+                start=(c == 0),
+                stop=(c == PASSES - 1),
+            )
+
+        def head_sums(s, t):
+            u, chunk = s // 2, s % 2
+            if chunk == 0 and t == 0:
+                sums[u] = sum_psum.tile([P, 2, units[u][2] // P, 4], F32, name="sum_bank")
+            toks = slice(t * P, (t + 1) * P)
+            heads = slice(2 * chunk, 2 * chunk + 2)
+            nc.tensor.matmul(sums[u][:, 0, t, heads], lhsT=product[s][:, toks], rhs=head_mask[:], start=True, stop=True)
+            nc.tensor.matmul(sums[u][:, 1, t, heads], lhsT=feature["q", s][:, toks],
+                             rhs=k_sum_heads[s][:, t // 2, :], start=True, stop=True)
+
+        def project_values(u, b):
+            g, first, width = units[u]
+            cols = slice(g * GROUP, (g + 1) * GROUP)
+            value[u, b] = value_psum.tile([P, 2, GROUP], F32, name="value_bank")
+            for t in range(2):
+                tok = first + b * S + t * P
+                for c in range(PASSES):
+                    nc.tensor.matmul_mx(
+                        out=value[u, b][:, t, :],
+                        lhsT=x_codes[:, c, tok:tok + P].bitcast(E5M2),
+                        lhsT_scale=x_scales[:, c, tok:tok + P],
+                        rhs=w_codes["v"][:, c, cols].bitcast(E4M3),
+                        rhs_scale=w_scales["v"][:, c, cols],
+                        start=(c == 0),
+                        stop=(c == PASSES - 1),
+                    )
+
+        def negative_part(w, s):
+            neg = work.tile([P, units[s // 2][2]], F32, name="negative")
+            nc.scalar.activation(out=neg[:], in_=proj[w, s][:], func=ACT.Relu, scale=-1.0)
+            return neg
+
+        def exponential(w, s, neg):
+            exp_part[w, s] = work.tile([P, units[s // 2][2]], F32, name="exp_part")
+            nc.scalar.activation(out=exp_part[w, s][:], in_=neg[:], func=ACT.Exp, scale=-1.0)
+
+        def feature_q(s):
+            feature["q", s] = work.tile([P, units[s // 2][2]], F32, name="feature_q")
+            nc.vector.scalar_tensor_tensor(out=feature["q", s][:], in0=proj["q", s][:], scalar=1.0,
+                                           in1=exp_part["q", s][:], op0=ALU.add, op1=ALU.max)
+
+        def feature_k(s):
+            feature["k", s] = work.tile([P, units[s // 2][2]], F32, name="feature_k")
+            batches = units[s // 2][2] // S
+            k_sum[s] = work.tile([P, batches], F32, name="k_sum")
+            for b in range(batches):
+                toks = slice(b * S, (b + 1) * S)
+                nc.vector.scalar_tensor_tensor(out=feature["k", s][:, toks], in0=proj["k", s][:, toks], scalar=1.0,
+                                               in1=exp_part["k", s][:, toks], op0=ALU.add, op1=ALU.max,
+                                               accum_out=k_sum[s][:, b:b + 1])
+
+        def split_k_sum(s):
+            shape = [P, units[s // 2][2] // S, 2]
+            k_sum_heads[s] = work.tile(shape, F32, name="k_sum_heads")
+            nc.gpsimd.tensor_tensor(out=k_sum_heads[s][:], in0=k_sum[s][:].unsqueeze(2).to_broadcast(shape),
+                                    in1=head_mask[:].unsqueeze(1).to_broadcast(shape), op=ALU.mult)
+
+        def multiply_qk(s, engine):
+            product[s] = work.tile([P, units[s // 2][2]], F32, name="product")
+            engine.tensor_tensor(out=product[s][:], in0=feature["q", s][:], in1=feature["k", s][:], op=ALU.mult)
+
+        def denominator(u):
+            den = work.tile([P, units[u][2] // 32], F32, name="den")
+            nc.scalar.activation(out=den[:], in_=sums[u][:, 1, :, :].rearrange("p t n -> p (t n)"),
+                                 func=ACT.Copy, bias=NORM_EPS)
+            return den
+
+        def invert(u, den):
+            inv = work.tile([P, units[u][2] // 32], F32, name="inv")
+            nc.vector.reciprocal(out=inv[:], in_=den[:])
+            return inv
+
+        def make_ratio(u, inv):
+            ratio[u] = work.tile([P, units[u][2] // 32], F32, name="ratio")
+            nc.vector.tensor_tensor(out=ratio[u][:], in0=sums[u][:, 0, :, :].rearrange("p t n -> p (t n)"),
+                                    in1=inv[:], op=ALU.mult)
+
+        def store(u, b, z):
+            g, first, width = units[u]
+            tok = first + b * S
+            rows = z_out[tok:tok + 2 * P, g * GROUP:(g + 1) * GROUP]
+            nc.sync.dma_start(out=rows.rearrange("(t p) n -> p t n", p=P), in_=z[:].rearrange("p (t n) d -> p t (n d)", t=2))
+
+        def scale_on_scalar(u, b):
+            z = work.tile([P, 8, DK], F32, name="z")
+            v = value[u, b][:].rearrange("p t (n d) -> p (t n) d", d=DK)
+            for j in range(8):
+                nc.scalar.activation(out=z[:, j, :], in_=v[:, j, :], func=ACT.Copy,
+                                     scale=ratio[u][:, 8 * b + j:8 * b + j + 1])
+            store(u, b, z)
+
+        def scale_on_vector(u, b):
+            z = work.tile([P, 8, DK], F32, name="z")
+            v = value[u, b][:].rearrange("p t (n d) -> p (t n) d", d=DK)
+            nc.vector.tensor_tensor(out=z[:], in0=v,
+                                    in1=ratio[u][:, 8 * b:8 * b + 8].unsqueeze(2).to_broadcast([P, 8, DK]), op=ALU.mult)
+            store(u, b, z)
+
+        def pieces(w, g):
+            return [(w, g, c) for c in range(PASSES)]
+
+        later = pieces("k", 1) + pieces("q", 1)
+        for g in range(2, GROUPS):
+            later += pieces("v", g - 2) + pieces("k", g) + pieces("q", g)
+        later += pieces("v", GROUPS - 2) + pieces("v", GROUPS - 1)
+
+        load_w(("k", 0, 0))
+        load_x(0)
+        load_x(1)
+        load_w(("k", 0, 1))
+        load_w(("q", 0, 0))
+        load_w(("q", 0, 1))
+        for t in range(2, 8):
+            load_x(t)
+        for piece in later:
+            load_w(piece)
+
+        on_scalar = [piece for piece in later if piece[0] == "v"][:SCALAR_PIECES]
+        mine = [piece for piece in later if piece not in on_scalar]
+        prep = [(interleave_w, mine[0])]
+        for n in range(1, len(mine)):
+            prep += [(interleave_w, mine[n]), (quantize_w, mine[n - 1])]
+        prep.append((quantize_w, mine[-1]))
+
+        def turn_and_copy(t):
+            copy_x(t, turn_x(t))
+
+        for t in range(2):
+            turn_and_copy(t)
+        interleave_w(("k", 0, 0))
+        quantize_w(("k", 0, 0))
+        interleave_w(("k", 0, 1))
+        quantize_x(0, 0)
+        quantize_w(("k", 0, 1))
+        quantize_x(0, 1)
+        interleave_w(("q", 0, 0))
+        interleave_w(("q", 0, 1))
+        quantize_w(("q", 0, 0))
+        quantize_w(("q", 0, 1))
+        for c in range(PASSES):
+            project_pass("k", 0, c)
+        exponential("k", 0, negative_part("k", 0))
+        feature_k(0)
+        split_k_sum(0)
+
+        tokens_done, prep_done, projected, scaled = 0, 0, 0, 0
+        for i in range(steps + SUM_LAG + 3):
+            has_q, has_k = i < steps, i + 1 < steps
+            sum_step = i - SUM_LAG
+            has_sums = 0 <= sum_step < steps
+            new_x = [2 * i + 2, 2 * i + 3] if i < 3 else []
+            to_scale = banks[scaled:projected]
+            to_scale = [ub for ub in to_scale if ub[0] in ratio]
+            if has_q:
+                tokens_done += units[i // 2][2]
+            turned = [turn_x(t) for t in new_x]
+            passes = [("q", i, c) for c in range(PASSES) if has_q] + [("k", i + 1, c) for c in range(PASSES) if has_k]
+            tiles = units[sum_step // 2][2] // P if has_sums else 0
+            for n in range(4):
+                if n < len(passes):
+                    project_pass(*passes[n])
+                if n < tiles and WEAVE:
+                    head_sums(sum_step, n)
+            if not WEAVE:
+                for n in range(tiles):
+                    head_sums(sum_step, n)
+            for t, bank in zip(new_x, turned):
+                copy_x(t, bank)
+            if has_q:
+                neg_q = negative_part("q", i)
+            if has_k:
+                neg_k = negative_part("k", i + 1)
+            if has_q:
+                exponential("q", i, neg_q)
+            if has_k:
+                exponential("k", i + 1, neg_k)
+            finished_unit = has_sums and sum_step % 2 == 1
+            if finished_unit:
+                den = denominator(sum_step // 2)
+            if 0 <= i - SCALAR_FROM < len(on_scalar):
+                interleave_w(on_scalar[i - SCALAR_FROM], True)
+            on_vector = []
+            for n, ub in enumerate(to_scale):
+                if scaled + n >= FIRST_VECTOR_BANK and (scaled + n) % VMOD == 0:
+                    on_vector.append(ub)
+                else:
+                    scale_on_scalar(*ub)
+            scaled += len(to_scale)
+            if new_x:
+                for c in range(PASSES):
+                    quantize_x(i + 1, c)
+            if has_q:
+                feature_q(i)
+                if G_FROM <= i < G_TO:
+                    multiply_qk(i, nc.gpsimd)
+            if has_k:
+                feature_k(i + 1)
+                split_k_sum(i + 1)
+            if has_q and not G_FROM <= i < G_TO:
+                multiply_qk(i, nc.vector)
+            for ub in on_vector:
+                scale_on_vector(*ub)
+            if finished_unit:
+                inv = invert(sum_step // 2, den)
+            if 0 <= i - SCALAR_FROM - 1 < len(on_scalar):
+                quantize_w(on_scalar[i - SCALAR_FROM - 1])
+            prep_to = min(len(prep), max(0, PREP_RATE * tokens_done // (2 * HALF) + PREP_HEAD))
+            for fn, piece in prep[prep_done:prep_to]:
+                fn(piece)
+            prep_done = max(prep_done, prep_to)
+            if finished_unit:
+                make_ratio(sum_step // 2, inv)
+            while projected < len(banks) and projected < scaled + 2 and (projected + VALUE_LAG <= tokens_done // HALF or not has_k):
+                project_values(*banks[projected])
+                projected += 1
+        assert scaled == len(banks) and prep_done == len(prep)

@@ -24,19 +24,16 @@ K_PASS = P * PACK
 PASSES = H // K_PASS
 GROUP = 256
 GROUPS = H // GROUP
-HALF = 512
+HEADS = GROUP // DK
+HEAD_ROWS = P // HEADS
+RUN = 4
+WIDE = 512
+
 SUM_LAG = 3
-VALUE_LAG = 7
-PREP_RATE = 5
-PREP_HEAD = 2
-FIRST_VECTOR_BANK = 8
-VMOD = 1
-G_FROM = 0
-G_TO = 0
-PROJ_BANKS = 4
-WEAVE = True
-SCALAR_PIECES = 4
-SCALAR_FROM = 3
+VALUE_LAG = 5
+CALLS_BEFORE_LOOP = 3
+CALLS_AHEAD = 5
+FIRST_VECTOR_SLAB = 10
 
 
 def tile_gatedlinearattention_pa_kernel(tc, hidden_states, Wq, Wk, Wv, out):
@@ -45,21 +42,29 @@ def tile_gatedlinearattention_pa_kernel(tc, hidden_states, Wq, Wk, Wv, out):
     z_out = out.rearrange("b s h -> (b s) h")
     weights = {"q": Wq, "k": Wk, "v": Wv}
 
+    units = [(g, tok, WIDE) for g in range(GROUPS) for tok in range(0, TOKENS, WIDE)][:-1]
+    units += [(GROUPS - 1, TOKENS - 2 * S, S), (GROUPS - 1, TOKENS - S, S)]
+    steps = 2 * len(units)
+    slabs = [(u, b) for u in range(len(units)) for b in range(units[u][2] // S)]
+
+    def tokens_of(s):
+        return units[s // 2][2]
+
     with ExitStack() as ctx:
         keep = ctx.enter_context(tc.tile_pool(name="keep", bufs=1))
-        stage = ctx.enter_context(tc.tile_pool(name="stage", bufs=4))
+        stage = ctx.enter_context(tc.tile_pool(name="stage", bufs=6))
         work = ctx.enter_context(tc.tile_pool(name="work", bufs=6))
-        proj_psum = ctx.enter_context(tc.psum_pool(name="proj", bufs=PROJ_BANKS))
+        proj_psum = ctx.enter_context(tc.psum_pool(name="proj", bufs=4))
         value_psum = ctx.enter_context(tc.psum_pool(name="value", bufs=2))
-        sum_psum = ctx.enter_context(tc.psum_pool(name="sums", bufs=6 - PROJ_BANKS))
+        sum_psum = ctx.enter_context(tc.psum_pool(name="sums", bufs=2))
         ctx.enter_context(tc.manual_schedule())
 
         identity = keep.tile([P, P], F32, name="identity")
         make_identity(nc, identity[:])
-        head_mask = keep.tile([P, 2], F32, name="head_mask")
+        head_mask = keep.tile([P, HEADS], F32, name="head_mask")
         nc.gpsimd.memset(head_mask[:], 0.0)
-        nc.gpsimd.memset(head_mask[0:DK, 0:1], 1.0)
-        nc.gpsimd.memset(head_mask[DK:P, 1:2], 1.0)
+        for n in range(HEADS):
+            nc.gpsimd.memset(head_mask[n * HEAD_ROWS:(n + 1) * HEAD_ROWS, n:n + 1], 1.0)
 
         x_codes = keep.tile([P, PASSES, TOKENS], U32, name="x_codes", align_bytes=64)
         x_scales = keep.tile([P, PASSES, TOKENS], U8, name="x_scales", align_bytes=64)
@@ -69,6 +74,9 @@ def tile_gatedlinearattention_pa_kernel(tc, hidden_states, Wq, Wk, Wv, out):
             w_scales[w] = keep.tile([P, PASSES, H], U8, name="scales_" + w, align_bytes=64)
 
         x_raw, w_raw, w_grouped, x_grouped = {}, {}, {}, {}
+        proj, exp_part, feature, k_sum, k_sum_heads, product, product_sum = {}, {}, {}, {}, {}, {}, {}
+        sums, ratio, value = {}, {}, {}
+
 
         def load_x(t):
             x_raw[t] = keep.tile([P, H], BF16, name="x_raw_%d" % t, align_bytes=64)
@@ -80,10 +88,14 @@ def tile_gatedlinearattention_pa_kernel(tc, hidden_states, Wq, Wk, Wv, out):
             rows = weights[w][c * K_PASS:(c + 1) * K_PASS, g * GROUP:(g + 1) * GROUP]
             nc.sync.dma_start(out=w_raw[piece][:], in_=rows.rearrange("(p j) n -> p j n", j=PACK))
 
-        def interleave_w(piece, on_scalar_engine=False):
+        def interleave_w(piece, copy=nc.vector.tensor_copy):
             w_grouped[piece] = stage.tile([P, GROUP, PACK], BF16, name="w_grouped", align_bytes=64)
-            copy = nc.scalar.copy if on_scalar_engine else nc.vector.tensor_copy
-            copy(out=w_grouped[piece][:], in_=w_raw[piece][:].rearrange("p j n -> p n j"))
+            if piece[0] == "v":
+                copy(out=w_grouped[piece][:].rearrange("p (e i) j -> p e j i", i=RUN),
+                     in_=w_raw[piece][:].rearrange("p j (e i) -> p e j i", i=RUN))
+            else:
+                copy(out=w_grouped[piece][:].rearrange("p (h e i) j -> p h e j i", h=2, i=RUN),
+                     in_=w_raw[piece][:].rearrange("p j (e h i) -> p h e j i", h=2, i=RUN))
 
         def quantize_w(piece):
             w, g, c = piece
@@ -94,47 +106,28 @@ def tile_gatedlinearattention_pa_kernel(tc, hidden_states, Wq, Wk, Wv, out):
                 in_=w_grouped[piece][:].rearrange("p n j -> p (n j)"),
             )
 
-        def turn_x(t):
+        def transpose_x(t):
             bank = value_psum.tile([P, PASSES, 2, P], F32, name="value_bank")
-            words = x_raw[t][:].bitcast(F32)
+            pairs = x_raw[t][:].bitcast(F32)
             for c in range(PASSES):
                 for u in range(2):
-                    nc.tensor.transpose(bank[:, c, u, :], words[:, 256 * c + u:256 * (c + 1):2], identity[:])
-            return bank
-
-        def copy_x(t, bank):
-            pair = t // 2
+                    nc.tensor.transpose(bank[:, c, u, :], pairs[:, 2 * P * c + u:2 * P * (c + 1):2], identity[:])
             if t % 2 == 0:
-                x_grouped[pair] = stage.tile([P, PASSES, 2, P, 2], F32, name="x_grouped", align_bytes=64)
-            nc.scalar.copy(out=x_grouped[pair][:, :, t % 2, :, :], in_=bank[:].rearrange("p c u r -> p c r u"))
+                x_grouped[t // 2] = stage.tile([P, PASSES, 2, P, 2], F32, name="x_grouped", align_bytes=64)
+            nc.scalar.copy(out=x_grouped[t // 2][:, :, t % 2, :, :], in_=bank[:].rearrange("p c u r -> p c r u"))
 
-        def quantize_x(pair, c):
-            cols = slice(pair * 2 * P, (pair + 1) * 2 * P)
+        def quantize_x(b, c):
+            cols = slice(b * S, (b + 1) * S)
             nc.vector.quantize_mx(
                 out=x_codes[:, c, cols].bitcast(E5M2),
                 scales=x_scales[:, c, cols],
-                in_=x_grouped[pair][:, c, :, :, :].rearrange("p t r u -> p (t r u)").bitcast(BF16),
+                in_=x_grouped[b][:, c, :, :, :].rearrange("p t r u -> p (t r u)").bitcast(BF16),
             )
 
-        units = []
-        for g in range(GROUPS):
-            for half in range(TOKENS // HALF):
-                if (g, half) in ((0, 0), (GROUPS - 1, 1)):
-                    units += [(g, half * HALF, S), (g, half * HALF + S, S)]
-                else:
-                    units.append((g, half * HALF, HALF))
-        steps = 2 * len(units)
-        banks = [(u, b) for u in range(len(units)) for b in range(units[u][2] // S)]
-
-        def step_place(s):
-            g, tok, width = units[s // 2]
-            return g * GROUP + (s % 2) * P, tok, width
-
-        proj, exp_part, feature, k_sum, k_sum_heads, product = {}, {}, {}, {}, {}, {}
-        sums, ratio, value = {}, {}, {}
 
         def project_pass(w, s, c):
-            col, tok, width = step_place(s)
+            g, tok, width = units[s // 2]
+            col = g * GROUP + (s % 2) * P
             if c == 0:
                 proj[w, s] = proj_psum.tile([P, width], F32, name="proj_bank")
             nc.tensor.matmul_mx(
@@ -147,103 +140,107 @@ def tile_gatedlinearattention_pa_kernel(tc, hidden_states, Wq, Wk, Wv, out):
                 stop=(c == PASSES - 1),
             )
 
-        def head_sums(s, t):
-            u, chunk = s // 2, s % 2
-            if chunk == 0 and t == 0:
-                sums[u] = sum_psum.tile([P, 2, units[u][2] // P, 4], F32, name="sum_bank")
-            toks = slice(t * P, (t + 1) * P)
-            heads = slice(2 * chunk, 2 * chunk + 2)
-            nc.tensor.matmul(sums[u][:, 0, t, heads], lhsT=product[s][:, toks], rhs=head_mask[:], start=True, stop=True)
-            nc.tensor.matmul(sums[u][:, 1, t, heads], lhsT=feature["q", s][:, toks],
-                             rhs=k_sum_heads[s][:, t // 2, :], start=True, stop=True)
-
-        def project_values(u, b):
+        def value_pass(n, pool, name, t, c):
+            u, b = slabs[n]
             g, first, width = units[u]
             cols = slice(g * GROUP, (g + 1) * GROUP)
-            value[u, b] = value_psum.tile([P, 2, GROUP], F32, name="value_bank")
-            for t in range(2):
-                tok = first + b * S + t * P
-                for c in range(PASSES):
-                    nc.tensor.matmul_mx(
-                        out=value[u, b][:, t, :],
-                        lhsT=x_codes[:, c, tok:tok + P].bitcast(E5M2),
-                        lhsT_scale=x_scales[:, c, tok:tok + P],
-                        rhs=w_codes["v"][:, c, cols].bitcast(E4M3),
-                        rhs_scale=w_scales["v"][:, c, cols],
-                        start=(c == 0),
-                        stop=(c == PASSES - 1),
-                    )
+            if t == 0 and c == 0:
+                value[n] = pool.tile([P, 2, GROUP], F32, name=name)
+            tok = first + b * S + t * P
+            nc.tensor.matmul_mx(
+                out=value[n][:, t, :],
+                lhsT=x_codes[:, c, tok:tok + P].bitcast(E5M2),
+                lhsT_scale=x_scales[:, c, tok:tok + P],
+                rhs=w_codes["v"][:, c, cols].bitcast(E4M3),
+                rhs_scale=w_scales["v"][:, c, cols],
+                start=(c == 0),
+                stop=(c == PASSES - 1),
+            )
+
+        def normalizer_sum(s, t):
+            u = s // 2
+            opens = s % 2 == 0 and t == 0
+            if opens:
+                sums[u] = sum_psum.tile([P, 2, tokens_of(s) // P, HEADS], F32, name="sum_bank")
+            nc.tensor.matmul(sums[u][:, 1, t, :], lhsT=feature["q", s][:, t * P:(t + 1) * P],
+                             rhs=k_sum_heads[s][:, t * P // S, :], start=opens, stop=False)
+
+        def qk_sum(u, t):
+            nc.tensor.matmul(sums[u][:, 0, t, :], lhsT=product_sum[u][:, t * P:(t + 1) * P], rhs=head_mask[:],
+                             start=False, stop=(t == units[u][2] // P - 1))
+
 
         def negative_part(w, s):
-            neg = work.tile([P, units[s // 2][2]], F32, name="negative")
-            nc.scalar.activation(out=neg[:], in_=proj[w, s][:], func=ACT.Relu, scale=-1.0)
-            return neg
+            negative = work.tile([P, tokens_of(s)], F32, name="negative")
+            nc.scalar.activation(out=negative[:], in_=proj[w, s][:], func=ACT.Relu, scale=-1.0)
+            return negative
 
-        def exponential(w, s, neg):
-            exp_part[w, s] = work.tile([P, units[s // 2][2]], F32, name="exp_part")
-            nc.scalar.activation(out=exp_part[w, s][:], in_=neg[:], func=ACT.Exp, scale=-1.0)
+        def exponential(w, s, negative):
+            exp_part[w, s] = work.tile([P, tokens_of(s)], F32, name="exp_part")
+            nc.scalar.activation(out=exp_part[w, s][:], in_=negative[:], func=ACT.Exp, scale=-1.0)
 
         def feature_q(s):
-            feature["q", s] = work.tile([P, units[s // 2][2]], F32, name="feature_q")
+            feature["q", s] = work.tile([P, tokens_of(s)], F32, name="feature_q")
             nc.vector.scalar_tensor_tensor(out=feature["q", s][:], in0=proj["q", s][:], scalar=1.0,
                                            in1=exp_part["q", s][:], op0=ALU.add, op1=ALU.max)
 
         def feature_k(s):
-            feature["k", s] = work.tile([P, units[s // 2][2]], F32, name="feature_k")
-            batches = units[s // 2][2] // S
+            batches = tokens_of(s) // S
+            feature["k", s] = work.tile([P, tokens_of(s)], F32, name="feature_k")
             k_sum[s] = work.tile([P, batches], F32, name="k_sum")
             for b in range(batches):
                 toks = slice(b * S, (b + 1) * S)
                 nc.vector.scalar_tensor_tensor(out=feature["k", s][:, toks], in0=proj["k", s][:, toks], scalar=1.0,
                                                in1=exp_part["k", s][:, toks], op0=ALU.add, op1=ALU.max,
                                                accum_out=k_sum[s][:, b:b + 1])
-
-        def split_k_sum(s):
-            shape = [P, units[s // 2][2] // S, 2]
+            shape = [P, batches, HEADS]
             k_sum_heads[s] = work.tile(shape, F32, name="k_sum_heads")
             nc.gpsimd.tensor_tensor(out=k_sum_heads[s][:], in0=k_sum[s][:].unsqueeze(2).to_broadcast(shape),
                                     in1=head_mask[:].unsqueeze(1).to_broadcast(shape), op=ALU.mult)
 
-        def multiply_qk(s, engine):
-            product[s] = work.tile([P, units[s // 2][2]], F32, name="product")
-            engine.tensor_tensor(out=product[s][:], in0=feature["q", s][:], in1=feature["k", s][:], op=ALU.mult)
+        def multiply_qk(s):
+            product[s] = work.tile([P, tokens_of(s)], F32, name="product")
+            nc.vector.tensor_tensor(out=product[s][:], in0=feature["q", s][:], in1=feature["k", s][:], op=ALU.mult)
+
+        def add_products(u, engine):
+            product_sum[u] = work.tile([P, units[u][2]], F32, name="product_sum")
+            engine.tensor_tensor(out=product_sum[u][:], in0=product[2 * u][:], in1=product[2 * u + 1][:], op=ALU.add)
+
 
         def denominator(u):
-            den = work.tile([P, units[u][2] // 32], F32, name="den")
+            den = work.tile([P, units[u][2] // P * HEADS], F32, name="den")
             nc.scalar.activation(out=den[:], in_=sums[u][:, 1, :, :].rearrange("p t n -> p (t n)"),
                                  func=ACT.Copy, bias=NORM_EPS)
             return den
 
         def invert(u, den):
-            inv = work.tile([P, units[u][2] // 32], F32, name="inv")
+            inv = work.tile([P, units[u][2] // P * HEADS], F32, name="inv")
             nc.vector.reciprocal(out=inv[:], in_=den[:])
             return inv
 
         def make_ratio(u, inv):
-            ratio[u] = work.tile([P, units[u][2] // 32], F32, name="ratio")
+            ratio[u] = work.tile([P, units[u][2] // P * HEADS], F32, name="ratio")
             nc.vector.tensor_tensor(out=ratio[u][:], in0=sums[u][:, 0, :, :].rearrange("p t n -> p (t n)"),
                                     in1=inv[:], op=ALU.mult)
 
-        def store(u, b, z):
+        def scale_and_store(n):
+            u, b = slabs[n]
             g, first, width = units[u]
+            factors = 2 * HEADS
+            z = work.tile([P, factors, DK], F32, name="z")
+            v = value[n][:].rearrange("p t (n d) -> p (t n) d", d=DK)
+            slab_ratio = ratio[u][:, factors * b:factors * (b + 1)]
+            if n < FIRST_VECTOR_SLAB:
+                for j in range(factors):
+                    nc.scalar.activation(out=z[:, j, :], in_=v[:, j, :], func=ACT.Copy, scale=slab_ratio[:, j:j + 1])
+            else:
+                nc.vector.tensor_tensor(out=z[:], in0=v, in1=slab_ratio.unsqueeze(2).to_broadcast([P, factors, DK]),
+                                        op=ALU.mult)
             tok = first + b * S
-            rows = z_out[tok:tok + 2 * P, g * GROUP:(g + 1) * GROUP]
-            nc.sync.dma_start(out=rows.rearrange("(t p) n -> p t n", p=P), in_=z[:].rearrange("p (t n) d -> p t (n d)", t=2))
+            rows = z_out[tok:tok + S, g * GROUP:(g + 1) * GROUP]
+            nc.sync.dma_start(out=rows.rearrange("(t p) n -> p t n", p=P),
+                              in_=z[:].rearrange("p (t n) d -> p t (n d)", t=2))
 
-        def scale_on_scalar(u, b):
-            z = work.tile([P, 8, DK], F32, name="z")
-            v = value[u, b][:].rearrange("p t (n d) -> p (t n) d", d=DK)
-            for j in range(8):
-                nc.scalar.activation(out=z[:, j, :], in_=v[:, j, :], func=ACT.Copy,
-                                     scale=ratio[u][:, 8 * b + j:8 * b + j + 1])
-            store(u, b, z)
-
-        def scale_on_vector(u, b):
-            z = work.tile([P, 8, DK], F32, name="z")
-            v = value[u, b][:].rearrange("p t (n d) -> p (t n) d", d=DK)
-            nc.vector.tensor_tensor(out=z[:], in0=v,
-                                    in1=ratio[u][:, 8 * b:8 * b + 8].unsqueeze(2).to_broadcast([P, 8, DK]), op=ALU.mult)
-            store(u, b, z)
 
         def pieces(w, g):
             return [(w, g, c) for c in range(PASSES)]
@@ -253,113 +250,120 @@ def tile_gatedlinearattention_pa_kernel(tc, hidden_states, Wq, Wk, Wv, out):
             later += pieces("v", g - 2) + pieces("k", g) + pieces("q", g)
         later += pieces("v", GROUPS - 2) + pieces("v", GROUPS - 1)
 
-        load_w(("k", 0, 0))
-        load_x(0)
-        load_x(1)
-        load_w(("k", 0, 1))
-        load_w(("q", 0, 0))
-        load_w(("q", 0, 1))
-        for t in range(2, 8):
+        for c in range(PASSES):
+            load_x(2 * c)
+            load_x(2 * c + 1)
+            load_w(("k", 0, c))
+        for piece in pieces("q", 0):
+            load_w(piece)
+        for t in range(WIDE // P, TOKENS // P):
             load_x(t)
         for piece in later:
             load_w(piece)
 
-        on_scalar = [piece for piece in later if piece[0] == "v"][:SCALAR_PIECES]
-        mine = [piece for piece in later if piece not in on_scalar]
-        prep = [(interleave_w, mine[0])]
-        for n in range(1, len(mine)):
-            prep += [(interleave_w, mine[n]), (quantize_w, mine[n - 1])]
-        prep.append((quantize_w, mine[-1]))
+        first_scalar = 2 * PASSES
+        scalar_pieces = later[first_scalar:first_scalar + VALUE_LAG - 1]
+        vector_pieces = [piece for piece in later if piece not in scalar_pieces]
+        calls = [(interleave_w, vector_pieces[0])]
+        for n in range(1, len(vector_pieces)):
+            calls += [(interleave_w, vector_pieces[n]), (quantize_w, vector_pieces[n - 1])]
+        calls.append((quantize_w, vector_pieces[-1]))
 
-        def turn_and_copy(t):
-            copy_x(t, turn_x(t))
+        def run_calls(first, last):
+            for fn, piece in calls[first:last]:
+                fn(piece)
 
-        for t in range(2):
-            turn_and_copy(t)
-        interleave_w(("k", 0, 0))
-        quantize_w(("k", 0, 0))
-        interleave_w(("k", 0, 1))
-        quantize_x(0, 0)
-        quantize_w(("k", 0, 1))
-        quantize_x(0, 1)
-        interleave_w(("q", 0, 0))
-        interleave_w(("q", 0, 1))
-        quantize_w(("q", 0, 0))
-        quantize_w(("q", 0, 1))
+        in_loop = steps - VALUE_LAG
+        project_turn = [n + VALUE_LAG if n < in_loop else steps + (n - in_loop) // 2 for n in range(len(slabs))]
+        scale_turn = [max(project_turn[n], 2 * slabs[n][0] + 1 + SUM_LAG) + 1 for n in range(len(slabs))]
+
+
+        for t in range(WIDE // P):
+            transpose_x(t)
+        for c in range(PASSES):
+            interleave_w(("k", 0, c))
+            quantize_x(c, 0)
+            quantize_w(("k", 0, c))
+            quantize_x(c, 1)
+        for piece in pieces("q", 0):
+            interleave_w(piece)
+        for piece in pieces("q", 0):
+            quantize_w(piece)
         for c in range(PASSES):
             project_pass("k", 0, c)
         exponential("k", 0, negative_part("k", 0))
+        transpose_x(4)
+        transpose_x(5)
         feature_k(0)
-        split_k_sum(0)
+        run_calls(0, 1)
+        for c in range(PASSES):
+            quantize_x(2, c)
+        run_calls(1, CALLS_BEFORE_LOOP)
+        calls_done = CALLS_BEFORE_LOOP
 
-        tokens_done, prep_done, projected, scaled = 0, 0, 0, 0
-        for i in range(steps + SUM_LAG + 3):
+
+        for i in range(scale_turn[-1] + 1):
             has_q, has_k = i < steps, i + 1 < steps
             sum_step = i - SUM_LAG
             has_sums = 0 <= sum_step < steps
-            new_x = [2 * i + 2, 2 * i + 3] if i < 3 else []
-            to_scale = banks[scaled:projected]
-            to_scale = [ub for ub in to_scale if ub[0] in ratio]
+            closes_unit = has_sums and sum_step % 2 == 1
+            sum_unit = sum_step // 2
+
+            wide = [(project_pass, ("q", i, c)) for c in range(PASSES) if has_q]
+            wide += [(project_pass, ("k", i + 1, c)) for c in range(PASSES) if has_k]
+            place = (value_psum, "value_bank") if has_q else (proj_psum, "proj_bank")
+            for n in range(len(slabs)):
+                if project_turn[n] == i:
+                    wide += [(value_pass, (n,) + place + (t, c)) for t in range(2) for c in range(PASSES)]
+            thin = []
+            if has_sums:
+                thin += [(normalizer_sum, (sum_step, t)) for t in range(tokens_of(sum_step) // P)]
+            if closes_unit:
+                thin += [(qk_sum, (sum_unit, t)) for t in range(tokens_of(sum_step) // P)]
+            for n in range(max(len(wide), len(thin))):
+                for fn, args in wide[n:n + 1] + thin[n:n + 1]:
+                    fn(*args)
+
             if has_q:
-                tokens_done += units[i // 2][2]
-            turned = [turn_x(t) for t in new_x]
-            passes = [("q", i, c) for c in range(PASSES) if has_q] + [("k", i + 1, c) for c in range(PASSES) if has_k]
-            tiles = units[sum_step // 2][2] // P if has_sums else 0
-            for n in range(4):
-                if n < len(passes):
-                    project_pass(*passes[n])
-                if n < tiles and WEAVE:
-                    head_sums(sum_step, n)
-            if not WEAVE:
-                for n in range(tiles):
-                    head_sums(sum_step, n)
-            for t, bank in zip(new_x, turned):
-                copy_x(t, bank)
-            if has_q:
-                neg_q = negative_part("q", i)
+                negative_q = negative_part("q", i)
             if has_k:
-                neg_k = negative_part("k", i + 1)
+                negative_k = negative_part("k", i + 1)
+            if i == 0:
+                transpose_x(6)
+                transpose_x(7)
             if has_q:
-                exponential("q", i, neg_q)
+                exponential("q", i, negative_q)
             if has_k:
-                exponential("k", i + 1, neg_k)
-            finished_unit = has_sums and sum_step % 2 == 1
-            if finished_unit:
-                den = denominator(sum_step // 2)
-            if 0 <= i - SCALAR_FROM < len(on_scalar):
-                interleave_w(on_scalar[i - SCALAR_FROM], True)
-            on_vector = []
-            for n, ub in enumerate(to_scale):
-                if scaled + n >= FIRST_VECTOR_BANK and (scaled + n) % VMOD == 0:
-                    on_vector.append(ub)
-                else:
-                    scale_on_scalar(*ub)
-            scaled += len(to_scale)
-            if new_x:
+                exponential("k", i + 1, negative_k)
+            if closes_unit:
+                den = denominator(sum_unit)
+            if 1 <= i <= len(scalar_pieces):
+                interleave_w(scalar_pieces[i - 1], nc.scalar.copy)
+            to_scale = [n for n in range(len(slabs)) if scale_turn[n] == i]
+            for n in to_scale:
+                if n < FIRST_VECTOR_SLAB:
+                    scale_and_store(n)
+
+            if i == 0:
                 for c in range(PASSES):
-                    quantize_x(i + 1, c)
+                    quantize_x(3, c)
             if has_q:
                 feature_q(i)
-                if G_FROM <= i < G_TO:
-                    multiply_qk(i, nc.gpsimd)
             if has_k:
                 feature_k(i + 1)
-                split_k_sum(i + 1)
-            if has_q and not G_FROM <= i < G_TO:
-                multiply_qk(i, nc.vector)
-            for ub in on_vector:
-                scale_on_vector(*ub)
-            if finished_unit:
-                inv = invert(sum_step // 2, den)
-            if 0 <= i - SCALAR_FROM - 1 < len(on_scalar):
-                quantize_w(on_scalar[i - SCALAR_FROM - 1])
-            prep_to = min(len(prep), max(0, PREP_RATE * tokens_done // (2 * HALF) + PREP_HEAD))
-            for fn, piece in prep[prep_done:prep_to]:
-                fn(piece)
-            prep_done = max(prep_done, prep_to)
-            if finished_unit:
-                make_ratio(sum_step // 2, inv)
-            while projected < len(banks) and projected < scaled + 2 and (projected + VALUE_LAG <= tokens_done // HALF or not has_k):
-                project_values(*banks[projected])
-                projected += 1
-        assert scaled == len(banks) and prep_done == len(prep)
+            for n in to_scale:
+                if n >= FIRST_VECTOR_SLAB:
+                    scale_and_store(n)
+            if closes_unit:
+                inv = invert(sum_unit, den)
+            if 2 <= i <= len(scalar_pieces) + 1:
+                quantize_w(scalar_pieces[i - 2])
+            calls_to = 2 * (i + 1) + CALLS_AHEAD
+            run_calls(calls_done, calls_to)
+            calls_done = calls_to
+            if closes_unit:
+                make_ratio(sum_unit, inv)
+            if has_q:
+                multiply_qk(i)
+            if has_q and i % 2 == 1:
+                add_products(i // 2, nc.gpsimd if has_k else nc.vector)

@@ -33,7 +33,7 @@ SUM_LAG = 3
 VALUE_LAG = 5
 CALLS_BEFORE_LOOP = 3
 CALLS_AHEAD = 5
-FIRST_VECTOR_SLAB = 10
+FIRST_VECTOR_SLAB = 12
 
 
 def tile_gatedlinearattention_pa_kernel(tc, hidden_states, Wq, Wk, Wv, out):
@@ -223,23 +223,24 @@ def tile_gatedlinearattention_pa_kernel(tc, hidden_states, Wq, Wk, Wv, out):
             nc.vector.tensor_tensor(out=ratio[u][:], in0=sums[u][:, 0, :, :].rearrange("p t n -> p (t n)"),
                                     in1=inv[:], op=ALU.mult)
 
-        def scale_and_store(n):
+        def scale_and_store(n, first_tile, tiles):
             u, b = slabs[n]
             g, first, width = units[u]
-            factors = 2 * HEADS
+            factors = tiles * HEADS
             z = work.tile([P, factors, DK], F32, name="z")
-            v = value[n][:].rearrange("p t (n d) -> p (t n) d", d=DK)
-            slab_ratio = ratio[u][:, factors * b:factors * (b + 1)]
+            v = value[n][:, first_tile:first_tile + tiles, :].rearrange("p t (n d) -> p (t n) d", d=DK)
+            first_factor = (2 * b + first_tile) * HEADS
+            tile_ratio = ratio[u][:, first_factor:first_factor + factors]
             if n < FIRST_VECTOR_SLAB:
                 for j in range(factors):
-                    nc.scalar.activation(out=z[:, j, :], in_=v[:, j, :], func=ACT.Copy, scale=slab_ratio[:, j:j + 1])
+                    nc.scalar.activation(out=z[:, j, :], in_=v[:, j, :], func=ACT.Copy, scale=tile_ratio[:, j:j + 1])
             else:
-                nc.vector.tensor_tensor(out=z[:], in0=v, in1=slab_ratio.unsqueeze(2).to_broadcast([P, factors, DK]),
+                nc.vector.tensor_tensor(out=z[:], in0=v, in1=tile_ratio.unsqueeze(2).to_broadcast([P, factors, DK]),
                                         op=ALU.mult)
-            tok = first + b * S
-            rows = z_out[tok:tok + S, g * GROUP:(g + 1) * GROUP]
+            tok = first + b * S + first_tile * P
+            rows = z_out[tok:tok + tiles * P, g * GROUP:(g + 1) * GROUP]
             nc.sync.dma_start(out=rows.rearrange("(t p) n -> p t n", p=P),
-                              in_=z[:].rearrange("p (t n) d -> p t (n d)", t=2))
+                              in_=z[:].rearrange("p (t n) d -> p t (n d)", t=tiles))
 
 
         def pieces(w, g):
@@ -324,6 +325,10 @@ def tile_gatedlinearattention_pa_kernel(tc, hidden_states, Wq, Wk, Wv, out):
                 for fn, args in wide[n:n + 1] + thin[n:n + 1]:
                     fn(*args)
 
+            to_scale = [n for n in range(len(slabs)) if scale_turn[n] == i]
+            for n in to_scale:
+                if n < FIRST_VECTOR_SLAB:
+                    scale_and_store(n, 0, 2)
             if has_q:
                 negative_q = negative_part("q", i)
             if has_k:
@@ -339,10 +344,6 @@ def tile_gatedlinearattention_pa_kernel(tc, hidden_states, Wq, Wk, Wv, out):
                 den = denominator(sum_unit)
             if 1 <= i <= len(scalar_pieces):
                 interleave_w(scalar_pieces[i - 1], nc.scalar.copy)
-            to_scale = [n for n in range(len(slabs)) if scale_turn[n] == i]
-            for n in to_scale:
-                if n < FIRST_VECTOR_SLAB:
-                    scale_and_store(n)
 
             if i == 0:
                 for c in range(PASSES):
@@ -352,8 +353,11 @@ def tile_gatedlinearattention_pa_kernel(tc, hidden_states, Wq, Wk, Wv, out):
             if has_k:
                 feature_k(i + 1)
             for n in to_scale:
-                if n >= FIRST_VECTOR_SLAB:
-                    scale_and_store(n)
+                if n == len(slabs) - 1:
+                    scale_and_store(n, 0, 1)
+                    scale_and_store(n, 1, 1)
+                elif n >= FIRST_VECTOR_SLAB:
+                    scale_and_store(n, 0, 2)
             if closes_unit:
                 inv = invert(sum_unit, den)
             if 2 <= i <= len(scalar_pieces) + 1:

from contextlib import ExitStack

import concourse.mybir as mybir
from concourse.masks import make_identity

B, S, H, NH = 4, 256, 1024, 16
DK = H // NH
NORM_EPS = 1e-6
TOKENS = B * S
FLOPS = 3 * 2 * TOKENS * H * H

F32 = mybir.dt.float32
BF16 = mybir.dt.bfloat16
U32 = mybir.dt.uint32
U8 = mybir.dt.uint8
E4M3 = mybir.dt.float8_e4m3fn_x4
E5M2 = mybir.dt.float8_e5m2_x4
ACT = mybir.ActivationFunctionType
ALU = mybir.AluOpType

P = 128
PACK = 4
K_PASS = P * PACK
PASSES = H // K_PASS
GROUP = 256
GROUPS = H // GROUP
HEADS = GROUP // DK
HEAD_ROWS = P // HEADS
RUN = 4
WIDE = 512

SUM_LAG = 3
VALUE_LAG = 5
CALLS_BEFORE_LOOP = 3
CALLS_AHEAD = 5
FIRST_VECTOR_SLAB = 12


def tile_gatedlinearattention_pa_kernel(tc, hidden_states, Wq, Wk, Wv, out):
    nc = tc.nc
    x = hidden_states.rearrange("b s h -> (b s) h")
    z_out = out.rearrange("b s h -> (b s) h")
    weights = {"q": Wq, "k": Wk, "v": Wv}

    units = [(g, tok, WIDE) for g in range(GROUPS) for tok in range(0, TOKENS, WIDE)][:-1]
    units += [(GROUPS - 1, TOKENS - 2 * S, S), (GROUPS - 1, TOKENS - S, S)]
    steps = 2 * len(units)
    slabs = [(u, b) for u in range(len(units)) for b in range(units[u][2] // S)]

    def tokens_of(s):
        return units[s // 2][2]

    with ExitStack() as ctx:
        keep = ctx.enter_context(tc.tile_pool(name="keep", bufs=1))
        stage = ctx.enter_context(tc.tile_pool(name="stage", bufs=6))
        work = ctx.enter_context(tc.tile_pool(name="work", bufs=6))
        proj_psum = ctx.enter_context(tc.psum_pool(name="proj", bufs=4))
        value_psum = ctx.enter_context(tc.psum_pool(name="value", bufs=2))
        sum_psum = ctx.enter_context(tc.psum_pool(name="sums", bufs=2))
        ctx.enter_context(tc.manual_schedule())

        identity = keep.tile([P, P], F32, name="identity")
        make_identity(nc, identity[:])
        head_mask = keep.tile([P, HEADS], F32, name="head_mask")
        nc.gpsimd.memset(head_mask[:], 0.0)
        for n in range(HEADS):
            nc.gpsimd.memset(head_mask[n * HEAD_ROWS:(n + 1) * HEAD_ROWS, n:n + 1], 1.0)

        x_codes = keep.tile([P, PASSES, TOKENS], U32, name="x_codes", align_bytes=64)
        x_scales = keep.tile([P, PASSES, TOKENS], U8, name="x_scales", align_bytes=64)
        w_codes, w_scales = {}, {}
        for w in "kqv":
            w_codes[w] = keep.tile([P, PASSES, H], U32, name="codes_" + w, align_bytes=64)
            w_scales[w] = keep.tile([P, PASSES, H], U8, name="scales_" + w, align_bytes=64)

        x_raw, w_raw, w_grouped, x_grouped = {}, {}, {}, {}
        proj, exp_part, feature, k_sum, k_sum_heads, product, product_sum = {}, {}, {}, {}, {}, {}, {}
        sums, ratio, value = {}, {}, {}


        def load_x(t):
            x_raw[t] = keep.tile([P, H], BF16, name="x_raw_%d" % t, align_bytes=64)
            nc.sync.dma_start(out=x_raw[t][:], in_=x[t * P:(t + 1) * P, :])

        def load_w(piece):
            w, g, c = piece
            w_raw[piece] = keep.tile([P, PACK, GROUP], BF16, name="raw_%s_%d_%d" % piece, align_bytes=64)
            rows = weights[w][c * K_PASS:(c + 1) * K_PASS, g * GROUP:(g + 1) * GROUP]
            nc.sync.dma_start(out=w_raw[piece][:], in_=rows.rearrange("(p j) n -> p j n", j=PACK))

        def interleave_w(piece, copy=nc.vector.tensor_copy):
            w_grouped[piece] = stage.tile([P, GROUP, PACK], BF16, name="w_grouped", align_bytes=64)
            if piece[0] == "v":
                copy(out=w_grouped[piece][:].rearrange("p (e i) j -> p e j i", i=RUN),
                     in_=w_raw[piece][:].rearrange("p j (e i) -> p e j i", i=RUN))
            else:
                copy(out=w_grouped[piece][:].rearrange("p (h e i) j -> p h e j i", h=2, i=RUN),
                     in_=w_raw[piece][:].rearrange("p j (e h i) -> p h e j i", h=2, i=RUN))

        def quantize_w(piece):
            w, g, c = piece
            cols = slice(g * GROUP, (g + 1) * GROUP)
            nc.vector.quantize_mx(
                out=w_codes[w][:, c, cols].bitcast(E4M3),
                scales=w_scales[w][:, c, cols],
                in_=w_grouped[piece][:].rearrange("p n j -> p (n j)"),
            )

        def transpose_x(t):
            bank = value_psum.tile([P, PASSES, 2, P], F32, name="value_bank")
            pairs = x_raw[t][:].bitcast(F32)
            for c in range(PASSES):
                for u in range(2):
                    nc.tensor.transpose(bank[:, c, u, :], pairs[:, 2 * P * c + u:2 * P * (c + 1):2], identity[:])
            if t % 2 == 0:
                x_grouped[t // 2] = stage.tile([P, PASSES, 2, P, 2], F32, name="x_grouped", align_bytes=64)
            nc.scalar.copy(out=x_grouped[t // 2][:, :, t % 2, :, :], in_=bank[:].rearrange("p c u r -> p c r u"))

        def quantize_x(b, c):
            cols = slice(b * S, (b + 1) * S)
            nc.vector.quantize_mx(
                out=x_codes[:, c, cols].bitcast(E5M2),
                scales=x_scales[:, c, cols],
                in_=x_grouped[b][:, c, :, :, :].rearrange("p t r u -> p (t r u)").bitcast(BF16),
            )


        def project_pass(w, s, c):
            g, tok, width = units[s // 2]
            col = g * GROUP + (s % 2) * P
            if c == 0:
                proj[w, s] = proj_psum.tile([P, width], F32, name="proj_bank")
            nc.tensor.matmul_mx(
                out=proj[w, s][:],
                lhsT=w_codes[w][:, c, col:col + P].bitcast(E4M3),
                lhsT_scale=w_scales[w][:, c, col:col + P],
                rhs=x_codes[:, c, tok:tok + width].bitcast(E5M2),
                rhs_scale=x_scales[:, c, tok:tok + width],
                start=(c == 0),
                stop=(c == PASSES - 1),
            )

        def value_pass(n, pool, name, t, c):
            u, b = slabs[n]
            g, first, width = units[u]
            cols = slice(g * GROUP, (g + 1) * GROUP)
            if t == 0 and c == 0:
                value[n] = pool.tile([P, 2, GROUP], F32, name=name)
            tok = first + b * S + t * P
            nc.tensor.matmul_mx(
                out=value[n][:, t, :],
                lhsT=x_codes[:, c, tok:tok + P].bitcast(E5M2),
                lhsT_scale=x_scales[:, c, tok:tok + P],
                rhs=w_codes["v"][:, c, cols].bitcast(E4M3),
                rhs_scale=w_scales["v"][:, c, cols],
                start=(c == 0),
                stop=(c == PASSES - 1),
            )

        def normalizer_sum(s, t):
            u = s // 2
            opens = s % 2 == 0 and t == 0
            if opens:
                sums[u] = sum_psum.tile([P, 2, tokens_of(s) // P, HEADS], F32, name="sum_bank")
            nc.tensor.matmul(sums[u][:, 1, t, :], lhsT=feature["q", s][:, t * P:(t + 1) * P],
                             rhs=k_sum_heads[s][:, t * P // S, :], start=opens, stop=False)

        def qk_sum(u, t):
            nc.tensor.matmul(sums[u][:, 0, t, :], lhsT=product_sum[u][:, t * P:(t + 1) * P], rhs=head_mask[:],
                             start=False, stop=(t == units[u][2] // P - 1))


        def negative_part(w, s):
            negative = work.tile([P, tokens_of(s)], F32, name="negative")
            nc.scalar.activation(out=negative[:], in_=proj[w, s][:], func=ACT.Relu, scale=-1.0)
            return negative

        def exponential(w, s, negative):
            exp_part[w, s] = work.tile([P, tokens_of(s)], F32, name="exp_part")
            nc.scalar.activation(out=exp_part[w, s][:], in_=negative[:], func=ACT.Exp, scale=-1.0)

        def feature_q(s):
            feature["q", s] = work.tile([P, tokens_of(s)], F32, name="feature_q")
            nc.vector.scalar_tensor_tensor(out=feature["q", s][:], in0=proj["q", s][:], scalar=1.0,
                                           in1=exp_part["q", s][:], op0=ALU.add, op1=ALU.max)

        def feature_k(s):
            batches = tokens_of(s) // S
            feature["k", s] = work.tile([P, tokens_of(s)], F32, name="feature_k")
            k_sum[s] = work.tile([P, batches], F32, name="k_sum")
            for b in range(batches):
                toks = slice(b * S, (b + 1) * S)
                nc.vector.scalar_tensor_tensor(out=feature["k", s][:, toks], in0=proj["k", s][:, toks], scalar=1.0,
                                               in1=exp_part["k", s][:, toks], op0=ALU.add, op1=ALU.max,
                                               accum_out=k_sum[s][:, b:b + 1])
            shape = [P, batches, HEADS]
            k_sum_heads[s] = work.tile(shape, F32, name="k_sum_heads")
            nc.gpsimd.tensor_tensor(out=k_sum_heads[s][:], in0=k_sum[s][:].unsqueeze(2).to_broadcast(shape),
                                    in1=head_mask[:].unsqueeze(1).to_broadcast(shape), op=ALU.mult)

        def multiply_qk(s):
            product[s] = work.tile([P, tokens_of(s)], F32, name="product")
            nc.vector.tensor_tensor(out=product[s][:], in0=feature["q", s][:], in1=feature["k", s][:], op=ALU.mult)

        def add_products(u, engine):
            product_sum[u] = work.tile([P, units[u][2]], F32, name="product_sum")
            engine.tensor_tensor(out=product_sum[u][:], in0=product[2 * u][:], in1=product[2 * u + 1][:], op=ALU.add)


        def denominator(u):
            den = work.tile([P, units[u][2] // P * HEADS], F32, name="den")
            nc.scalar.activation(out=den[:], in_=sums[u][:, 1, :, :].rearrange("p t n -> p (t n)"),
                                 func=ACT.Copy, bias=NORM_EPS)
            return den

        def invert(u, den):
            inv = work.tile([P, units[u][2] // P * HEADS], F32, name="inv")
            nc.vector.reciprocal(out=inv[:], in_=den[:])
            return inv

        def make_ratio(u, inv):
            ratio[u] = work.tile([P, units[u][2] // P * HEADS], F32, name="ratio")
            nc.vector.tensor_tensor(out=ratio[u][:], in0=sums[u][:, 0, :, :].rearrange("p t n -> p (t n)"),
                                    in1=inv[:], op=ALU.mult)

        def scale_and_store(n, first_tile, tiles):
            u, b = slabs[n]
            g, first, width = units[u]
            factors = tiles * HEADS
            z = work.tile([P, factors, DK], F32, name="z")
            v = value[n][:, first_tile:first_tile + tiles, :].rearrange("p t (n d) -> p (t n) d", d=DK)
            first_factor = (2 * b + first_tile) * HEADS
            tile_ratio = ratio[u][:, first_factor:first_factor + factors]
            if n < FIRST_VECTOR_SLAB:
                for j in range(factors):
                    nc.scalar.activation(out=z[:, j, :], in_=v[:, j, :], func=ACT.Copy, scale=tile_ratio[:, j:j + 1])
            else:
                nc.vector.tensor_tensor(out=z[:], in0=v, in1=tile_ratio.unsqueeze(2).to_broadcast([P, factors, DK]),
                                        op=ALU.mult)
            tok = first + b * S + first_tile * P
            rows = z_out[tok:tok + tiles * P, g * GROUP:(g + 1) * GROUP]
            nc.sync.dma_start(out=rows.rearrange("(t p) n -> p t n", p=P),
                              in_=z[:].rearrange("p (t n) d -> p t (n d)", t=tiles))


        def pieces(w, g):
            return [(w, g, c) for c in range(PASSES)]

        later = pieces("k", 1) + pieces("q", 1)
        for g in range(2, GROUPS):
            later += pieces("v", g - 2) + pieces("k", g) + pieces("q", g)
        later += pieces("v", GROUPS - 2) + pieces("v", GROUPS - 1)

        for c in range(PASSES):
            load_x(2 * c)
            load_x(2 * c + 1)
            load_w(("k", 0, c))
        for piece in pieces("q", 0):
            load_w(piece)
        for t in range(WIDE // P, TOKENS // P):
            load_x(t)
        for piece in later:
            load_w(piece)

        first_scalar = 2 * PASSES
        scalar_pieces = later[first_scalar:first_scalar + VALUE_LAG - 1]
        vector_pieces = [piece for piece in later if piece not in scalar_pieces]
        calls = [(interleave_w, vector_pieces[0])]
        for n in range(1, len(vector_pieces)):
            calls += [(interleave_w, vector_pieces[n]), (quantize_w, vector_pieces[n - 1])]
        calls.append((quantize_w, vector_pieces[-1]))

        def run_calls(first, last):
            for fn, piece in calls[first:last]:
                fn(piece)

        in_loop = steps - VALUE_LAG
        project_turn = [n + VALUE_LAG if n < in_loop else steps + (n - in_loop) // 2 for n in range(len(slabs))]
        scale_turn = [max(project_turn[n], 2 * slabs[n][0] + 1 + SUM_LAG) + 1 for n in range(len(slabs))]


        for t in range(WIDE // P):
            transpose_x(t)
        for c in range(PASSES):
            interleave_w(("k", 0, c))
            quantize_x(c, 0)
            quantize_w(("k", 0, c))
            quantize_x(c, 1)
        for piece in pieces("q", 0):
            interleave_w(piece)
        for piece in pieces("q", 0):
            quantize_w(piece)
        for c in range(PASSES):
            project_pass("k", 0, c)
        exponential("k", 0, negative_part("k", 0))
        transpose_x(4)
        transpose_x(5)
        feature_k(0)
        run_calls(0, 1)
        for c in range(PASSES):
            quantize_x(2, c)
        run_calls(1, CALLS_BEFORE_LOOP)
        calls_done = CALLS_BEFORE_LOOP


        for i in range(scale_turn[-1] + 1):
            has_q, has_k = i < steps, i + 1 < steps
            sum_step = i - SUM_LAG
            has_sums = 0 <= sum_step < steps
            closes_unit = has_sums and sum_step % 2 == 1
            sum_unit = sum_step // 2

            wide = [(project_pass, ("q", i, c)) for c in range(PASSES) if has_q]
            wide += [(project_pass, ("k", i + 1, c)) for c in range(PASSES) if has_k]
            place = (value_psum, "value_bank") if has_q else (proj_psum, "proj_bank")
            for n in range(len(slabs)):
                if project_turn[n] == i:
                    wide += [(value_pass, (n,) + place + (t, c)) for t in range(2) for c in range(PASSES)]
            thin = []
            if has_sums:
                thin += [(normalizer_sum, (sum_step, t)) for t in range(tokens_of(sum_step) // P)]
            if closes_unit:
                thin += [(qk_sum, (sum_unit, t)) for t in range(tokens_of(sum_step) // P)]
            for n in range(max(len(wide), len(thin))):
                for fn, args in wide[n:n + 1] + thin[n:n + 1]:
                    fn(*args)

            to_scale = [n for n in range(len(slabs)) if scale_turn[n] == i]
            for n in to_scale:
                if n < FIRST_VECTOR_SLAB:
                    scale_and_store(n, 0, 2)
            if has_q:
                negative_q = negative_part("q", i)
            if has_k:
                negative_k = negative_part("k", i + 1)
            if i == 0:
                transpose_x(6)
                transpose_x(7)
            if has_q:
                exponential("q", i, negative_q)
            if has_k:
                exponential("k", i + 1, negative_k)
            if closes_unit:
                den = denominator(sum_unit)
            if 1 <= i <= len(scalar_pieces):
                interleave_w(scalar_pieces[i - 1], nc.scalar.copy)

            if i == 0:
                for c in range(PASSES):
                    quantize_x(3, c)
            if has_q:
                feature_q(i)
            if has_k:
                feature_k(i + 1)
            for n in to_scale:
                if n == len(slabs) - 1:
                    scale_and_store(n, 0, 1)
                    scale_and_store(n, 1, 1)
                elif n >= FIRST_VECTOR_SLAB:
                    scale_and_store(n, 0, 2)
            if closes_unit:
                inv = invert(sum_unit, den)
            if 2 <= i <= len(scalar_pieces) + 1:
                quantize_w(scalar_pieces[i - 2])
            calls_to = 2 * (i + 1) + CALLS_AHEAD
            run_calls(calls_done, calls_to)
            calls_done = calls_to
            if closes_unit:
                make_ratio(sum_unit, inv)
            if has_q:
                multiply_qk(i)
            if has_q and i % 2 == 1:
                add_products(i // 2, nc.gpsimd if has_k else nc.vector)
